import numpy as np
import ml_dtypes


def mxq(x, axis, fmt="e4m3"):
    dtype, down = {"e4m3": (ml_dtypes.float8_e4m3fn, 7), "e5m2": (ml_dtypes.float8_e5m2, 14)}[fmt]
    v = np.moveaxis(np.asarray(x, np.float32).astype(ml_dtypes.bfloat16).astype(np.float64), axis, -1)
    blocks = v.reshape(v.shape[:-1] + (-1, 32))
    amax = np.abs(blocks).max(-1, keepdims=True)
    byte = np.maximum(np.where(amax > 0, np.frexp(amax)[1] - 1 + 127, 0) - down, 1)
    scale = np.exp2(byte - 127.0)
    codes = (blocks / scale).astype(np.float32).astype(dtype).astype(np.float64)
    return np.moveaxis((codes * scale).reshape(v.shape), -1, axis)


WIDE = False


def mx_kscale(k):
    if not WIDE:
        return np.ones(k)
    levels = np.array([10, -10, 5, -5, 0])
    if k % 512:
        return np.exp2(np.random.permutation(np.resize(levels, k // 32))).repeat(32)
    a = np.empty((k // 512, 16))
    for p in range(k // 512):
        a[p, :8] = np.random.permutation(np.resize(levels, 8))
        for g in range(8):
            far = levels[np.abs(levels - a[p, g]) >= 10]
            a[p, g + 8] = far[np.random.randint(len(far))]
    return np.exp2(a.ravel()).repeat(32)


BF16 = ml_dtypes.bfloat16


def bf(x):
    return np.asarray(x, np.float32).astype(BF16)


def f64(x):
    return np.asarray(x).astype(np.float64)


B, N0, N1, N2, N3, T, K = 256, 512, 1024, 1024, 512, 8, 512
R = min(K, N0, N1)
R2 = min(R, T)
GS = 0.25


def setup_inputs():
    s, t = mx_kscale(R), mx_kscale(R)
    return {"S": bf(np.random.standard_normal((R, R, R2)) * s[:, None, None] * t[None, :, None]),
            "U0": bf(np.random.standard_normal((N1, R)) / np.sqrt(R) / s[None, :]),
            "U1": bf(np.random.standard_normal((N0, R)) * GS / np.sqrt(R) / t[None, :])}


def reference(S, U0, U1):
    w1 = mxq(f64(S).reshape(R, R * R2).T, 1, "e4m3") @ mxq(f64(U0).T, 0, "e4m3")
    w2 = mxq(w1.reshape(R, R2 * N1).T, 1, "e4m3") @ mxq(f64(U1).T, 0, "e4m3")
    return w2.reshape(R2, N1, N0)

@@ -1,0 +1,240 @@
+from contextlib import ExitStack
+
+import concourse.mybir as mybir
+from concourse.masks import make_identity
+
+BF16 = mybir.dt.bfloat16
+F32 = mybir.dt.float32
+U32 = mybir.dt.uint32
+U8 = mybir.dt.uint8
+FP8X4 = mybir.dt.float8_e4m3fn_x4
+
+P = 128
+PACK = 4
+K = P * PACK
+R = 8
+J = 1024
+I = 512
+J_BLOCKS = J // P
+FACTOR_BLOCKS = 4
+R_HALF = R // 2
+UNIT = 4
+STORE_BANKS = 2
+STORES_IN_FLIGHT = 8
+BANKS = R * J_BLOCKS
+PSUM_BANKS = 8
+LAG = PSUM_BANKS
+SCALAR_SHARE = 8
+
+FLOPS = 2 * K * (K * R) * J + 2 * K * (R * J) * I
+
+
+def bank_indices(n):
+    j_half, rest = divmod(n, BANKS // 2)
+    r, place = divmod(rest, FACTOR_BLOCKS)
+    return r, j_half * FACTOR_BLOCKS + place
+
+
+def quantise_u0_blocks(nc, psum, stage, identity, rows, codes, scales):
+    grouped = stage.tile([P, FACTOR_BLOCKS * P * PACK], BF16, align_bytes=64, name="u0_grouped")
+    grouped_words = grouped[:].bitcast(F32).rearrange("x (b a u) -> x b a u", b=FACTOR_BLOCKS, u=2)
+    for first in range(0, FACTOR_BLOCKS, 2):
+        flipped = psum.tile([P, 2, 2, P], F32, name="u0_flipped", tag="one")
+        for b in range(2):
+            words = rows[:, first + b, :].bitcast(F32)
+            for u in range(2):
+                nc.tensor.transpose(flipped[:, b, u, :], words[:, u::2], identity)
+        source = flipped[:].rearrange("x b u a -> x b a u")
+        if first == 0:
+            nc.vector.tensor_copy(out=grouped_words[:, first : first + 2], in_=source)
+        else:
+            nc.scalar.copy(out=grouped_words[:, first : first + 2], in_=source)
+    nc.vector.quantize_mx(out=codes.bitcast(FP8X4), scales=scales, in_=grouped[:])
+
+
+def quantise_u1(nc, psum, stage, identity, rows, codes, scales):
+    grouped = stage.tile([P, FACTOR_BLOCKS, P, PACK], BF16, align_bytes=64, name="u1_grouped")
+    for b in range(FACTOR_BLOCKS):
+        flipped = psum.tile([P, PACK, P], BF16, name="u1_flipped", tag="two")
+        for t in range(PACK):
+            nc.tensor.transpose(flipped[:, t, :], rows[:, b, t::PACK], identity)
+        source = flipped[:].rearrange("y t a -> y a t")
+        if b % 2 == 0:
+            nc.vector.tensor_copy(out=grouped[:, b], in_=source)
+        else:
+            nc.scalar.copy(out=grouped[:, b], in_=source)
+    nc.vector.quantize_mx(
+        out=codes.bitcast(FP8X4),
+        scales=scales,
+        in_=grouped[:].rearrange("y b a t -> y (b a t)"),
+    )
+
+
+def tile_mtl_net_tf_pa_kernel(tc, S, U0, U1, out):
+    nc = tc.nc
+    with ExitStack() as ctx:
+        keep = ctx.enter_context(tc.tile_pool(name="keep", bufs=1))
+        stage = ctx.enter_context(tc.tile_pool(name="stage", bufs=3))
+        psum = ctx.enter_context(tc.psum_pool(name="psum", bufs=PSUM_BANKS // 2))
+
+        u0_view = U0.rearrange("(a b) q -> a b q", b=J_BLOCKS)
+        u0_rows = keep.tile([P, J_BLOCKS, K], BF16)
+        first_half = slice(0, FACTOR_BLOCKS)
+        second_half = slice(FACTOR_BLOCKS, J_BLOCKS)
+        u1_rows = keep.tile([P, FACTOR_BLOCKS, K], BF16)
+        s_view = S.rearrange("(x t) p r -> x t p r", t=PACK)
+        s_raw = []
+        for c in range(PACK):
+            raw = keep.tile([P, PACK, P, R], BF16, name="s_raw%d" % c)
+            nc.sync.dma_start(out=raw[:], in_=s_view[:, :, c * P : (c + 1) * P, :])
+            s_raw.append(raw)
+            if c == 0:
+                nc.sync.dma_start(out=u0_rows[:, first_half, :], in_=u0_view[:, first_half, :])
+                nc.sync.dma_start(out=u1_rows[:], in_=U1.rearrange("(b a) p -> a b p", a=P))
+        nc.sync.dma_start(out=u0_rows[:, second_half, :], in_=u0_view[:, second_half, :])
+
+        identity_words = keep.tile([P, P], F32)
+        make_identity(nc, identity_words[:])
+        identity = keep.tile([P, P], BF16)
+        make_identity(nc, identity[:])
+
+        u0_codes = keep.tile([P, J_BLOCKS, P], U32, align_bytes=64)
+        u0_scales = keep.tile([P, J_BLOCKS, P], U8, align_bytes=64)
+        u1_codes = keep.tile([P, I], U32, align_bytes=64)
+        u1_scales = keep.tile([P, I], U8, align_bytes=64)
+        s_codes = keep.tile([P, R, PACK * P], U32, align_bytes=64)
+        s_scales = keep.tile([P, R, PACK * P], U8, align_bytes=64)
+        s_grouped = [
+            keep.tile([P, R_HALF, PACK, P, PACK], BF16, align_bytes=64, name="s_grouped%d" % half)
+            for half in range(2)
+        ]
+        w1_bank = {}
+        w1_grouped = {}
+        w1_codes = {}
+        w1_scales = {}
+        result = {}
+        out_view = out.rearrange("r (a b) i -> r a b i", b=J_BLOCKS)
+
+        def quantise_u0_half(blocks):
+            quantise_u0_blocks(
+                nc,
+                psum,
+                stage,
+                identity_words[:],
+                u0_rows[:, blocks, :],
+                u0_codes[:, blocks, :].rearrange("x b a -> x (b a)"),
+                u0_scales[:, blocks, :].rearrange("x b a -> x (b a)"),
+            )
+
+        def regroup_s(c):
+            for half in range(2):
+                rows = slice(c * P // PACK, (c + 1) * P // PACK)
+                target = s_grouped[half][:, :, :, rows, :].rearrange("x r k y t -> x k y t r")
+                source = s_raw[c][:, :, :, half * R_HALF : (half + 1) * R_HALF].rearrange(
+                    "x t (y k) r -> x k y t r", k=PACK
+                )
+                if half == 0:
+                    nc.vector.tensor_copy(out=target, in_=source)
+                else:
+                    nc.scalar.copy(out=target, in_=source)
+
+        def quantise_s(r):
+            half, r_low = divmod(r, R_HALF)
+            nc.vector.quantize_mx(
+                out=s_codes[:, r, :].bitcast(FP8X4),
+                scales=s_scales[:, r, :],
+                in_=s_grouped[half][:, r_low].rearrange("x k y t -> x (k y t)"),
+            )
+
+        def w1_pass(n, c):
+            r, b = bank_indices(n)
+            if c == 0:
+                early_second_tag = PSUM_BANKS // 2 <= n < PSUM_BANKS
+                w1_bank[n] = psum.tile(
+                    [P, PACK, P], F32, name="w1_bank", tag="two" if early_second_tag else "one"
+                )
+            nc.tensor.matmul_mx(
+                out=w1_bank[n][:, c, :],
+                lhsT=s_codes[:, r, c * P : (c + 1) * P].bitcast(FP8X4),
+                lhsT_scale=s_scales[:, r, c * P : (c + 1) * P],
+                rhs=u0_codes[:, b, :].bitcast(FP8X4),
+                rhs_scale=u0_scales[:, b, :],
+                start=True,
+                stop=True,
+            )
+
+        def round_w1(n):
+            unit, place = divmod(n, UNIT)
+            if place == 0:
+                w1_grouped[unit] = stage.tile(
+                    [P, UNIT, P, PACK], BF16, align_bytes=64, name="w1_grouped"
+                )
+            source = w1_bank[n][:].rearrange("y c a -> y a c")
+            if n % SCALAR_SHARE == SCALAR_SHARE - 1 or (n < LAG and n % UNIT != 0):
+                nc.scalar.copy(out=w1_grouped[unit][:, place], in_=source)
+            else:
+                nc.vector.tensor_copy(out=w1_grouped[unit][:, place], in_=source)
+
+        def quantise_w1(unit):
+            w1_codes[unit] = stage.tile([P, UNIT * P], U32, align_bytes=64, name="w1_codes")
+            w1_scales[unit] = stage.tile([P, UNIT * P], U8, align_bytes=64, name="w1_scales")
+            nc.vector.quantize_mx(
+                out=w1_codes[unit][:].bitcast(FP8X4),
+                scales=w1_scales[unit][:],
+                in_=w1_grouped[unit][:].rearrange("y u a c -> y (u a c)"),
+            )
+
+        def second_contraction(n):
+            r, b = bank_indices(n)
+            unit, place = divmod(n, UNIT)
+            batch, slot = divmod(n, STORE_BANKS)
+            if slot == 0:
+                result[batch] = stage.tile(
+                    [P, STORE_BANKS, I], F32, name="result", bufs=STORES_IN_FLIGHT
+                )
+            out_bank = psum.tile([P, I], F32, name="out_bank", tag="two")
+            nc.tensor.matmul_mx(
+                out=out_bank[:],
+                lhsT=w1_codes[unit][:, place * P : (place + 1) * P].bitcast(FP8X4),
+                lhsT_scale=w1_scales[unit][:, place * P : (place + 1) * P],
+                rhs=u1_codes[:].bitcast(FP8X4),
+                rhs_scale=u1_scales[:],
+                start=True,
+                stop=True,
+            )
+            if n >= BANKS - LAG and n % 2 == 1:
+                nc.vector.tensor_copy(out=result[batch][:, slot, :], in_=out_bank[:])
+            else:
+                nc.scalar.copy(out=result[batch][:, slot, :], in_=out_bank[:])
+            if slot == STORE_BANKS - 1:
+                nc.sync.dma_start(out=out_view[r, :, b - slot : b + 1, :], in_=result[batch][:])
+
+        def step(n):
+            if PSUM_BANKS <= n < BANKS:
+                for c in range(PACK):
+                    w1_pass(n, c)
+            if n < BANKS:
+                round_w1(n)
+            if n % UNIT == 0 and UNIT <= n <= BANKS:
+                quantise_w1(n // UNIT - 1)
+            if n % FACTOR_BLOCKS == 1 and n // FACTOR_BLOCKS + 2 < R:
+                quantise_s(n // FACTOR_BLOCKS + 2)
+            if n >= LAG:
+                second_contraction(n - LAG)
+
+        for c in range(PACK):
+            regroup_s(c)
+            if c == 0:
+                quantise_u0_half(first_half)
+                quantise_u1(nc, psum, stage, identity[:], u1_rows, u1_codes[:], u1_scales[:])
+        for r in range(2):
+            quantise_s(r)
+        for n in range(PSUM_BANKS):
+            for c in range(PACK):
+                w1_pass(n, c)
+
+        for n in range(LAG):
+            step(n)
+        quantise_u0_half(second_half)
+        for n in range(LAG, BANKS + LAG):
+            step(n)

@@ -18,56 +18,40 @@ I = 512
 J_BLOCKS = J // P
 FACTOR_BLOCKS = 4
 R_HALF = R // 2
+S_CHUNKS = (128, 128, 128, 64, 64)
 UNIT = 4
 STORE_BANKS = 2
 STORES_IN_FLIGHT = 8
 BANKS = R * J_BLOCKS
 PSUM_BANKS = 8
-LAG = PSUM_BANKS
-SCALAR_SHARE = 8
+LAG = 8
+SCALAR_SHARE = 5
 
 FLOPS = 2 * K * (K * R) * J + 2 * K * (R * J) * I
 
 
 def bank_indices(n):
-    j_half, rest = divmod(n, BANKS // 2)
-    r, place = divmod(rest, FACTOR_BLOCKS)
-    return r, j_half * FACTOR_BLOCKS + place
+    r_half, rest = divmod(n, BANKS // 2)
+    j_half, rest = divmod(rest, BANKS // 4)
+    r_low, place = divmod(rest, FACTOR_BLOCKS)
+    return r_half * R_HALF + r_low, j_half * FACTOR_BLOCKS + place
 
 
-def quantise_u0_blocks(nc, psum, stage, identity, rows, codes, scales):
-    grouped = stage.tile([P, FACTOR_BLOCKS * P * PACK], BF16, align_bytes=64, name="u0_grouped")
+def quantise_factor(nc, psum, tag, stage, identity, rows, codes, scales):
+    grouped = stage.tile([P, FACTOR_BLOCKS * P * PACK], BF16, align_bytes=64, name="factor_grouped")
     grouped_words = grouped[:].bitcast(F32).rearrange("x (b a u) -> x b a u", b=FACTOR_BLOCKS, u=2)
     for first in range(0, FACTOR_BLOCKS, 2):
-        flipped = psum.tile([P, 2, 2, P], F32, name="u0_flipped", tag="one")
+        flipped = psum.tile([P, 2, 2, P], F32, name="factor_flipped", tag=tag)
         for b in range(2):
             words = rows[:, first + b, :].bitcast(F32)
             for u in range(2):
                 nc.tensor.transpose(flipped[:, b, u, :], words[:, u::2], identity)
         source = flipped[:].rearrange("x b u a -> x b a u")
-        if first == 0:
+        if first == 0 and tag == "one":
             nc.vector.tensor_copy(out=grouped_words[:, first : first + 2], in_=source)
         else:
             nc.scalar.copy(out=grouped_words[:, first : first + 2], in_=source)
     nc.vector.quantize_mx(out=codes.bitcast(FP8X4), scales=scales, in_=grouped[:])
-
-
-def quantise_u1(nc, psum, stage, identity, rows, codes, scales):
-    grouped = stage.tile([P, FACTOR_BLOCKS, P, PACK], BF16, align_bytes=64, name="u1_grouped")
-    for b in range(FACTOR_BLOCKS):
-        flipped = psum.tile([P, PACK, P], BF16, name="u1_flipped", tag="two")
-        for t in range(PACK):
-            nc.tensor.transpose(flipped[:, t, :], rows[:, b, t::PACK], identity)
-        source = flipped[:].rearrange("y t a -> y a t")
-        if b % 2 == 0:
-            nc.vector.tensor_copy(out=grouped[:, b], in_=source)
-        else:
-            nc.scalar.copy(out=grouped[:, b], in_=source)
-    nc.vector.quantize_mx(
-        out=codes.bitcast(FP8X4),
-        scales=scales,
-        in_=grouped[:].rearrange("y b a t -> y (b a t)"),
-    )
 
 
 def tile_mtl_net_tf_pa_kernel(tc, S, U0, U1, out):
@@ -84,18 +68,19 @@ def tile_mtl_net_tf_pa_kernel(tc, S, U0, U1, out):
         u1_rows = keep.tile([P, FACTOR_BLOCKS, K], BF16)
         s_view = S.rearrange("(x t) p r -> x t p r", t=PACK)
         s_raw = []
-        for c in range(PACK):
-            raw = keep.tile([P, PACK, P, R], BF16, name="s_raw%d" % c)
-            nc.sync.dma_start(out=raw[:], in_=s_view[:, :, c * P : (c + 1) * P, :])
+        s_first = []
+        for c, width in enumerate(S_CHUNKS):
+            p0 = sum(S_CHUNKS[:c])
+            raw = keep.tile([P, PACK, width, R], BF16, name="s_raw%d" % c)
+            nc.sync.dma_start(out=raw[:], in_=s_view[:, :, p0 : p0 + width, :])
             s_raw.append(raw)
+            s_first.append(p0)
             if c == 0:
                 nc.sync.dma_start(out=u0_rows[:, first_half, :], in_=u0_view[:, first_half, :])
-                nc.sync.dma_start(out=u1_rows[:], in_=U1.rearrange("(b a) p -> a b p", a=P))
+        nc.sync.dma_start(out=u1_rows[:], in_=U1.rearrange("(b a) p -> a b p", a=P))
         nc.sync.dma_start(out=u0_rows[:, second_half, :], in_=u0_view[:, second_half, :])
 
-        identity_words = keep.tile([P, P], F32)
-        make_identity(nc, identity_words[:])
-        identity = keep.tile([P, P], BF16)
+        identity = keep.tile([P, P], F32)
         make_identity(nc, identity[:])
 
         u0_codes = keep.tile([P, J_BLOCKS, P], U32, align_bytes=64)
@@ -116,11 +101,12 @@ def tile_mtl_net_tf_pa_kernel(tc, S, U0, U1, out):
         out_view = out.rearrange("r (a b) i -> r a b i", b=J_BLOCKS)
 
         def quantise_u0_half(blocks):
-            quantise_u0_blocks(
+            quantise_factor(
                 nc,
                 psum,
+                "one",
                 stage,
-                identity_words[:],
+                identity[:],
                 u0_rows[:, blocks, :],
                 u0_codes[:, blocks, :].rearrange("x b a -> x (b a)"),
                 u0_scales[:, blocks, :].rearrange("x b a -> x (b a)"),
@@ -128,12 +114,12 @@ def tile_mtl_net_tf_pa_kernel(tc, S, U0, U1, out):
 
         def regroup_s(c):
             for half in range(2):
-                rows = slice(c * P // PACK, (c + 1) * P // PACK)
-                target = s_grouped[half][:, :, :, rows, :].rearrange("x r k y t -> x k y t r")
+                y_run = slice(s_first[c] // PACK, (s_first[c] + S_CHUNKS[c]) // PACK)
+                target = s_grouped[half][:, :, :, y_run, :].rearrange("x r k y t -> x k y t r")
                 source = s_raw[c][:, :, :, half * R_HALF : (half + 1) * R_HALF].rearrange(
                     "x t (y k) r -> x k y t r", k=PACK
                 )
-                if half == 0:
+                if half == 0 or c == 1:
                     nc.vector.tensor_copy(out=target, in_=source)
                 else:
                     nc.scalar.copy(out=target, in_=source)
@@ -146,22 +132,19 @@ def tile_mtl_net_tf_pa_kernel(tc, S, U0, U1, out):
                 in_=s_grouped[half][:, r_low].rearrange("x k y t -> x (k y t)"),
             )
 
-        def w1_pass(n, c):
+        def first_contraction(n):
             r, b = bank_indices(n)
-            if c == 0:
-                early_second_tag = PSUM_BANKS // 2 <= n < PSUM_BANKS
-                w1_bank[n] = psum.tile(
-                    [P, PACK, P], F32, name="w1_bank", tag="two" if early_second_tag else "one"
+            w1_bank[n] = psum.tile([P, PACK, P], F32, name="w1_bank", tag="one")
+            for k in range(PACK):
+                nc.tensor.matmul_mx(
+                    out=w1_bank[n][:, k, :],
+                    lhsT=s_codes[:, r, k * P : (k + 1) * P].bitcast(FP8X4),
+                    lhsT_scale=s_scales[:, r, k * P : (k + 1) * P],
+                    rhs=u0_codes[:, b, :].bitcast(FP8X4),
+                    rhs_scale=u0_scales[:, b, :],
+                    start=True,
+                    stop=True,
                 )
-            nc.tensor.matmul_mx(
-                out=w1_bank[n][:, c, :],
-                lhsT=s_codes[:, r, c * P : (c + 1) * P].bitcast(FP8X4),
-                lhsT_scale=s_scales[:, r, c * P : (c + 1) * P],
-                rhs=u0_codes[:, b, :].bitcast(FP8X4),
-                rhs_scale=u0_scales[:, b, :],
-                start=True,
-                stop=True,
-            )
 
         def round_w1(n):
             unit, place = divmod(n, UNIT)
@@ -169,7 +152,7 @@ def tile_mtl_net_tf_pa_kernel(tc, S, U0, U1, out):
                 w1_grouped[unit] = stage.tile(
                     [P, UNIT, P, PACK], BF16, align_bytes=64, name="w1_grouped"
                 )
-            source = w1_bank[n][:].rearrange("y c a -> y a c")
+            source = w1_bank[n][:].rearrange("y k a -> y a k")
             if n % SCALAR_SHARE == SCALAR_SHARE - 1 or (n < LAG and n % UNIT != 0):
                 nc.scalar.copy(out=w1_grouped[unit][:, place], in_=source)
             else:
@@ -181,7 +164,7 @@ def tile_mtl_net_tf_pa_kernel(tc, S, U0, U1, out):
             nc.vector.quantize_mx(
                 out=w1_codes[unit][:].bitcast(FP8X4),
                 scales=w1_scales[unit][:],
-                in_=w1_grouped[unit][:].rearrange("y u a c -> y (u a c)"),
+                in_=w1_grouped[unit][:].rearrange("y u a k -> y (u a k)"),
             )
 
         def second_contraction(n):
@@ -209,32 +192,26 @@ def tile_mtl_net_tf_pa_kernel(tc, S, U0, U1, out):
             if slot == STORE_BANKS - 1:
                 nc.sync.dma_start(out=out_view[r, :, b - slot : b + 1, :], in_=result[batch][:])
 
-        def step(n):
-            if PSUM_BANKS <= n < BANKS:
-                for c in range(PACK):
-                    w1_pass(n, c)
-            if n < BANKS:
-                round_w1(n)
-            if n % UNIT == 0 and UNIT <= n <= BANKS:
-                quantise_w1(n // UNIT - 1)
-            if n % FACTOR_BLOCKS == 1 and n // FACTOR_BLOCKS + 2 < R:
-                quantise_s(n // FACTOR_BLOCKS + 2)
-            if n >= LAG:
-                second_contraction(n - LAG)
-
-        for c in range(PACK):
+        for c in range(len(S_CHUNKS)):
             regroup_s(c)
             if c == 0:
                 quantise_u0_half(first_half)
-                quantise_u1(nc, psum, stage, identity[:], u1_rows, u1_codes[:], u1_scales[:])
-        for r in range(2):
-            quantise_s(r)
-        for n in range(PSUM_BANKS):
-            for c in range(PACK):
-                w1_pass(n, c)
+        quantise_s(0)
+        quantise_factor(nc, psum, "two", stage, identity[:], u1_rows[:], u1_codes[:], u1_scales[:])
 
-        for n in range(LAG):
-            step(n)
-        quantise_u0_half(second_half)
-        for n in range(LAG, BANKS + LAG):
-            step(n)
+        for n in range(BANKS + LAG):
+            if n < BANKS:
+                first_contraction(n)
+                round_w1(n)
+            if n % UNIT == 0 and UNIT <= n <= BANKS:
+                quantise_w1(n // UNIT - 1)
+            if n % UNIT == 1 and n < BANKS and bank_indices(n)[1] < FACTOR_BLOCKS:
+                r_next = bank_indices(n)[0] + 1
+                if r_next % R_HALF != 0:
+                    quantise_s(r_next)
+            if n == BANKS // 2 - UNIT:
+                quantise_s(R_HALF)
+            if n == 2 * UNIT:
+                quantise_u0_half(second_half)
+            if n >= LAG:
+                second_contraction(n - LAG)

@@ -18,16 +18,28 @@ I = 512
 J_BLOCKS = J // P
 FACTOR_BLOCKS = 4
 R_HALF = R // 2
-S_CHUNKS = (128, 128, 128, 64, 64)
+S_CHUNKS = (128, 128, 128, 128)
 UNIT = 4
+SCALAR_CHUNKS = 3
+WARM_UP_COLUMNS = 512
+WARM_UP = {2: 5, 3: 4}
 STORE_BANKS = 2
 STORES_IN_FLIGHT = 8
 BANKS = R * J_BLOCKS
+UNIT_LAST = list(range(UNIT - 1, BANKS - UNIT, UNIT)) + [BANKS - UNIT // 2 - 1, BANKS - 1]
 PSUM_BANKS = 8
 LAG = 8
-SCALAR_SHARE = 5
+SCALAR_SHARE = 4
+VECTOR_ONLY = BANKS - 12
+SCALAR_EARLY = range(1, LAG)
 
 FLOPS = 2 * K * (K * R) * J + 2 * K * (R * J) * I
+
+
+def unit_indices(n):
+    unit = sum(1 for last in UNIT_LAST if last < n)
+    first = UNIT_LAST[unit - 1] + 1 if unit > 0 else 0
+    return unit, n - first, UNIT_LAST[unit] + 1 - first
 
 
 def bank_indices(n):
@@ -112,17 +124,32 @@ def tile_mtl_net_tf_pa_kernel(tc, S, U0, U1, out):
                 u0_scales[:, blocks, :].rearrange("x b a -> x (b a)"),
             )
 
-        def regroup_s(c):
-            for half in range(2):
-                y_run = slice(s_first[c] // PACK, (s_first[c] + S_CHUNKS[c]) // PACK)
-                target = s_grouped[half][:, :, :, y_run, :].rearrange("x r k y t -> x k y t r")
-                source = s_raw[c][:, :, :, half * R_HALF : (half + 1) * R_HALF].rearrange(
-                    "x t (y k) r -> x k y t r", k=PACK
+        def regroup_s(c, engine, r_first, r_count, k_first=0, k_count=PACK):
+            half, r_low = divmod(r_first, R_HALF)
+            y_run = slice(s_first[c] // PACK, (s_first[c] + S_CHUNKS[c]) // PACK)
+            k_run = slice(k_first, k_first + k_count)
+            target = s_grouped[half][:, r_low : r_low + r_count, k_run, y_run, :].rearrange(
+                "x r k y t -> x k y t r"
+            )
+            source = s_raw[c][:, :, :, r_first : r_first + r_count].rearrange(
+                "x t (y k) r -> x k y t r", k=PACK
+            )[:, k_run]
+            if engine == "vector":
+                nc.vector.tensor_copy(out=target, in_=source)
+            else:
+                nc.scalar.copy(out=target, in_=source)
+
+        def warm_up(c, count):
+            idle_bank = psum.tile([P, WARM_UP_COLUMNS], F32, name="idle_bank", tag="two")
+            for t in range(count):
+                flat = s_raw[c][:, t % PACK].rearrange("x p r -> x (p r)")
+                nc.tensor.matmul(
+                    idle_bank[:],
+                    lhsT=flat[:, :P],
+                    rhs=flat[:, :WARM_UP_COLUMNS],
+                    start=True,
+                    stop=True,
                 )
-                if half == 0 or c == 1:
-                    nc.vector.tensor_copy(out=target, in_=source)
-                else:
-                    nc.scalar.copy(out=target, in_=source)
 
         def quantise_s(r):
             half, r_low = divmod(r, R_HALF)
@@ -147,20 +174,21 @@ def tile_mtl_net_tf_pa_kernel(tc, S, U0, U1, out):
                 )
 
         def round_w1(n):
-            unit, place = divmod(n, UNIT)
+            unit, place, count = unit_indices(n)
             if place == 0:
                 w1_grouped[unit] = stage.tile(
-                    [P, UNIT, P, PACK], BF16, align_bytes=64, name="w1_grouped"
+                    [P, count, P, PACK], BF16, align_bytes=64, name="w1_grouped"
                 )
             source = w1_bank[n][:].rearrange("y k a -> y a k")
-            if n % SCALAR_SHARE == SCALAR_SHARE - 1 or (n < LAG and n % UNIT != 0):
+            if (n < VECTOR_ONLY and n % SCALAR_SHARE == SCALAR_SHARE - 1) or n in SCALAR_EARLY:
                 nc.scalar.copy(out=w1_grouped[unit][:, place], in_=source)
             else:
                 nc.vector.tensor_copy(out=w1_grouped[unit][:, place], in_=source)
 
         def quantise_w1(unit):
-            w1_codes[unit] = stage.tile([P, UNIT * P], U32, align_bytes=64, name="w1_codes")
-            w1_scales[unit] = stage.tile([P, UNIT * P], U8, align_bytes=64, name="w1_scales")
+            count = unit_indices(UNIT_LAST[unit])[2]
+            w1_codes[unit] = stage.tile([P, count * P], U32, align_bytes=64, name="w1_codes")
+            w1_scales[unit] = stage.tile([P, count * P], U8, align_bytes=64, name="w1_scales")
             nc.vector.quantize_mx(
                 out=w1_codes[unit][:].bitcast(FP8X4),
                 scales=w1_scales[unit][:],
@@ -169,7 +197,7 @@ def tile_mtl_net_tf_pa_kernel(tc, S, U0, U1, out):
 
         def second_contraction(n):
             r, b = bank_indices(n)
-            unit, place = divmod(n, UNIT)
+            unit, place = unit_indices(n)[:2]
             batch, slot = divmod(n, STORE_BANKS)
             if slot == 0:
                 result[batch] = stage.tile(
@@ -189,11 +217,17 @@ def tile_mtl_net_tf_pa_kernel(tc, S, U0, U1, out):
                 nc.vector.tensor_copy(out=result[batch][:, slot, :], in_=out_bank[:])
             else:
                 nc.scalar.copy(out=result[batch][:, slot, :], in_=out_bank[:])
-            if slot == STORE_BANKS - 1:
+            if n >= BANKS - UNIT:
+                nc.sync.dma_start(out=out_view[r, :, b, :], in_=result[batch][:, slot, :])
+            elif slot == STORE_BANKS - 1:
                 nc.sync.dma_start(out=out_view[r, :, b - slot : b + 1, :], in_=result[batch][:])
 
         for c in range(len(S_CHUNKS)):
-            regroup_s(c)
+            regroup_s(c, "vector", 0, R_HALF)
+            if c < SCALAR_CHUNKS:
+                regroup_s(c, "scalar", R_HALF, R_HALF)
+            if c in WARM_UP:
+                warm_up(c, WARM_UP[c])
             if c == 0:
                 quantise_u0_half(first_half)
         quantise_s(0)
@@ -203,14 +237,16 @@ def tile_mtl_net_tf_pa_kernel(tc, S, U0, U1, out):
             if n < BANKS:
                 first_contraction(n)
                 round_w1(n)
-            if n % UNIT == 0 and UNIT <= n <= BANKS:
-                quantise_w1(n // UNIT - 1)
+            if n - 1 in UNIT_LAST:
+                quantise_w1(UNIT_LAST.index(n - 1))
             if n % UNIT == 1 and n < BANKS and bank_indices(n)[1] < FACTOR_BLOCKS:
                 r_next = bank_indices(n)[0] + 1
                 if r_next % R_HALF != 0:
                     quantise_s(r_next)
             if n == BANKS // 2 - UNIT:
                 quantise_s(R_HALF)
+            if 2 * UNIT <= n < 3 * UNIT:
+                regroup_s(SCALAR_CHUNKS, "vector", R_HALF, R_HALF, n - 2 * UNIT, 1)
             if n == 2 * UNIT:
                 quantise_u0_half(second_half)
             if n >= LAG:

@@ -22,16 +22,15 @@ S_CHUNKS = (128, 128, 128, 128)
 UNIT = 4
 SCALAR_CHUNKS = 3
 WARM_UP_COLUMNS = 512
-WARM_UP = {2: 5, 3: 4}
+WARM_UP = {2: 5, 3: 3}
 STORE_BANKS = 2
 STORES_IN_FLIGHT = 8
 BANKS = R * J_BLOCKS
-UNIT_LAST = list(range(UNIT - 1, BANKS - UNIT, UNIT)) + [BANKS - UNIT // 2 - 1, BANKS - 1]
+UNIT_LAST = list(range(UNIT - 1, BANKS, UNIT))
 PSUM_BANKS = 8
 LAG = 8
-SCALAR_SHARE = 4
-VECTOR_ONLY = BANKS - 12
-SCALAR_EARLY = range(1, LAG)
+SCALAR_SHARE = 5
+SCALAR_EARLY = (1, 3, 4, 5, 6, 7)
 
 FLOPS = 2 * K * (K * R) * J + 2 * K * (R * J) * I
 
@@ -59,7 +58,7 @@ def quantise_factor(nc, psum, tag, stage, identity, rows, codes, scales):
             for u in range(2):
                 nc.tensor.transpose(flipped[:, b, u, :], words[:, u::2], identity)
         source = flipped[:].rearrange("x b u a -> x b a u")
-        if first == 0 and tag == "one":
+        if first == 0:
             nc.vector.tensor_copy(out=grouped_words[:, first : first + 2], in_=source)
         else:
             nc.scalar.copy(out=grouped_words[:, first : first + 2], in_=source)
@@ -180,7 +179,7 @@ def tile_mtl_net_tf_pa_kernel(tc, S, U0, U1, out):
                     [P, count, P, PACK], BF16, align_bytes=64, name="w1_grouped"
                 )
             source = w1_bank[n][:].rearrange("y k a -> y a k")
-            if (n < VECTOR_ONLY and n % SCALAR_SHARE == SCALAR_SHARE - 1) or n in SCALAR_EARLY:
+            if n % SCALAR_SHARE == SCALAR_SHARE - 1 or n in SCALAR_EARLY:
                 nc.scalar.copy(out=w1_grouped[unit][:, place], in_=source)
             else:
                 nc.vector.tensor_copy(out=w1_grouped[unit][:, place], in_=source)
@@ -217,23 +216,10 @@ def tile_mtl_net_tf_pa_kernel(tc, S, U0, U1, out):
                 nc.vector.tensor_copy(out=result[batch][:, slot, :], in_=out_bank[:])
             else:
                 nc.scalar.copy(out=result[batch][:, slot, :], in_=out_bank[:])
-            if n >= BANKS - UNIT:
-                nc.sync.dma_start(out=out_view[r, :, b, :], in_=result[batch][:, slot, :])
-            elif slot == STORE_BANKS - 1:
+            if slot == STORE_BANKS - 1:
                 nc.sync.dma_start(out=out_view[r, :, b - slot : b + 1, :], in_=result[batch][:])
 
-        for c in range(len(S_CHUNKS)):
-            regroup_s(c, "vector", 0, R_HALF)
-            if c < SCALAR_CHUNKS:
-                regroup_s(c, "scalar", R_HALF, R_HALF)
-            if c in WARM_UP:
-                warm_up(c, WARM_UP[c])
-            if c == 0:
-                quantise_u0_half(first_half)
-        quantise_s(0)
-        quantise_factor(nc, psum, "two", stage, identity[:], u1_rows[:], u1_codes[:], u1_scales[:])
-
-        for n in range(BANKS + LAG):
+        def contraction_step(n):
             if n < BANKS:
                 first_contraction(n)
                 round_w1(n)
@@ -251,3 +237,25 @@ def tile_mtl_net_tf_pa_kernel(tc, S, U0, U1, out):
                 quantise_u0_half(second_half)
             if n >= LAG:
                 second_contraction(n - LAG)
+
+        with tc.manual_schedule(engines={mybir.EngineType.PE}):
+            for c in range(len(S_CHUNKS)):
+                if c < SCALAR_CHUNKS:
+                    regroup_s(c, "vector", 0, R_HALF)
+                    regroup_s(c, "scalar", R_HALF, R_HALF)
+                else:
+                    regroup_s(c, "vector", 0, R_HALF // 2)
+                    regroup_s(c, "scalar", R_HALF // 2, R_HALF // 2)
+                if c in WARM_UP:
+                    warm_up(c, WARM_UP[c])
+                if c == 0:
+                    quantise_u0_half(first_half)
+            quantise_s(0)
+            for n in range(UNIT):
+                contraction_step(n)
+            quantise_factor(
+                nc, psum, "two", stage, identity[:], u1_rows[:], u1_codes[:], u1_scales[:]
+            )
+
+        for n in range(UNIT, BANKS + LAG):
+            contraction_step(n)

@@ -21,6 +21,9 @@ R_HALF = R // 2
 S_CHUNKS = (128, 128, 128, 128)
 UNIT = 4
 SCALAR_CHUNKS = 3
+Y_PART = P // 2
+EARLY_R = 2
+U0_SECOND = 11
 WARM_UP_COLUMNS = 512
 WARM_UP = {2: 5, 3: 3}
 STORE_BANKS = 2
@@ -29,8 +32,8 @@ BANKS = R * J_BLOCKS
 UNIT_LAST = list(range(UNIT - 1, BANKS, UNIT))
 PSUM_BANKS = 8
 LAG = 8
-SCALAR_SHARE = 5
-SCALAR_EARLY = (1, 3, 4, 5, 6, 7)
+SCALAR_SHARE = 4
+SCALAR_EARLY = (1, 3, 4, 5)
 
 FLOPS = 2 * K * (K * R) * J + 2 * K * (R * J) * I
 
@@ -48,7 +51,7 @@ def bank_indices(n):
     return r_half * R_HALF + r_low, j_half * FACTOR_BLOCKS + place
 
 
-def quantise_factor(nc, psum, tag, stage, identity, rows, codes, scales):
+def turn_factor(nc, psum, tag, stage, identity, rows, copies):
     grouped = stage.tile([P, FACTOR_BLOCKS * P * PACK], BF16, align_bytes=64, name="factor_grouped")
     grouped_words = grouped[:].bitcast(F32).rearrange("x (b a u) -> x b a u", b=FACTOR_BLOCKS, u=2)
     for first in range(0, FACTOR_BLOCKS, 2):
@@ -57,12 +60,9 @@ def quantise_factor(nc, psum, tag, stage, identity, rows, codes, scales):
             words = rows[:, first + b, :].bitcast(F32)
             for u in range(2):
                 nc.tensor.transpose(flipped[:, b, u, :], words[:, u::2], identity)
-        source = flipped[:].rearrange("x b u a -> x b a u")
-        if first == 0:
-            nc.vector.tensor_copy(out=grouped_words[:, first : first + 2], in_=source)
-        else:
-            nc.scalar.copy(out=grouped_words[:, first : first + 2], in_=source)
-    nc.vector.quantize_mx(out=codes.bitcast(FP8X4), scales=scales, in_=grouped[:])
+        copy = copies[first // 2]
+        copy(out=grouped_words[:, first : first + 2], in_=flipped[:].rearrange("x b u a -> x b a u"))
+    return grouped
 
 
 def tile_mtl_net_tf_pa_kernel(tc, S, U0, U1, out):
@@ -111,16 +111,11 @@ def tile_mtl_net_tf_pa_kernel(tc, S, U0, U1, out):
         result = {}
         out_view = out.rearrange("r (a b) i -> r a b i", b=J_BLOCKS)
 
-        def quantise_u0_half(blocks):
-            quantise_factor(
-                nc,
-                psum,
-                "one",
-                stage,
-                identity[:],
-                u0_rows[:, blocks, :],
-                u0_codes[:, blocks, :].rearrange("x b a -> x (b a)"),
-                u0_scales[:, blocks, :].rearrange("x b a -> x (b a)"),
+        def quantise_u0_half(grouped, blocks):
+            nc.vector.quantize_mx(
+                out=u0_codes[:, blocks, :].rearrange("x b a -> x (b a)").bitcast(FP8X4),
+                scales=u0_scales[:, blocks, :].rearrange("x b a -> x (b a)"),
+                in_=grouped[:],
             )
 
         def regroup_s(c, engine, r_first, r_count, k_first=0, k_count=PACK):
@@ -158,6 +153,18 @@ def tile_mtl_net_tf_pa_kernel(tc, S, U0, U1, out):
                 in_=s_grouped[half][:, r_low].rearrange("x k y t -> x (k y t)"),
             )
 
+        def quantise_s_part(r, y_first):
+            half, r_low = divmod(r, R_HALF)
+            for k in range(PACK):
+                columns = slice(k * P + y_first, k * P + y_first + Y_PART)
+                nc.vector.quantize_mx(
+                    out=s_codes[:, r, columns].bitcast(FP8X4),
+                    scales=s_scales[:, r, columns],
+                    in_=s_grouped[half][:, r_low, k, y_first : y_first + Y_PART, :].rearrange(
+                        "x y t -> x (y t)"
+                    ),
+                )
+
         def first_contraction(n):
             r, b = bank_indices(n)
             w1_bank[n] = psum.tile([P, PACK, P], F32, name="w1_bank", tag="one")
@@ -179,7 +186,9 @@ def tile_mtl_net_tf_pa_kernel(tc, S, U0, U1, out):
                     [P, count, P, PACK], BF16, align_bytes=64, name="w1_grouped"
                 )
             source = w1_bank[n][:].rearrange("y k a -> y a k")
-            if n % SCALAR_SHARE == SCALAR_SHARE - 1 or n in SCALAR_EARLY:
+            if n >= UNIT:
+                nc.any.tensor_copy(out=w1_grouped[unit][:, place], in_=source)
+            elif n % 2 == 1:
                 nc.scalar.copy(out=w1_grouped[unit][:, place], in_=source)
             else:
                 nc.vector.tensor_copy(out=w1_grouped[unit][:, place], in_=source)
@@ -212,50 +221,73 @@ def tile_mtl_net_tf_pa_kernel(tc, S, U0, U1, out):
                 start=True,
                 stop=True,
             )
-            if n >= BANKS - LAG and n % 2 == 1:
-                nc.vector.tensor_copy(out=result[batch][:, slot, :], in_=out_bank[:])
-            else:
-                nc.scalar.copy(out=result[batch][:, slot, :], in_=out_bank[:])
+            nc.any.tensor_copy(out=result[batch][:, slot, :], in_=out_bank[:])
             if slot == STORE_BANKS - 1:
                 nc.sync.dma_start(out=out_view[r, :, b - slot : b + 1, :], in_=result[batch][:])
 
+        both = (nc.vector.tensor_copy, nc.scalar.copy)
+
         def contraction_step(n):
+            if n >= LAG:
+                second_contraction(n - LAG)
             if n < BANKS:
                 first_contraction(n)
                 round_w1(n)
-            if n - 1 in UNIT_LAST:
+            if n - 1 in UNIT_LAST and n > UNIT:
                 quantise_w1(UNIT_LAST.index(n - 1))
-            if n % UNIT == 1 and n < BANKS and bank_indices(n)[1] < FACTOR_BLOCKS:
+            if n % UNIT == 1 and UNIT < n < BANKS and bank_indices(n)[1] < FACTOR_BLOCKS:
                 r_next = bank_indices(n)[0] + 1
                 if r_next % R_HALF != 0:
                     quantise_s(r_next)
-            if n == BANKS // 2 - UNIT:
+            if n == BANKS // 2 - 2 * UNIT:
                 quantise_s(R_HALF)
             if 2 * UNIT <= n < 3 * UNIT:
                 regroup_s(SCALAR_CHUNKS, "vector", R_HALF, R_HALF, n - 2 * UNIT, 1)
-            if n == 2 * UNIT:
-                quantise_u0_half(second_half)
-            if n >= LAG:
-                second_contraction(n - LAG)
+            if n == U0_SECOND:
+                quantise_u0_half(
+                    turn_factor(
+                        nc, psum, "one", stage, identity[:], u0_rows[:, second_half, :], both
+                    ),
+                    second_half,
+                )
 
-        with tc.manual_schedule(engines={mybir.EngineType.PE}):
+        with tc.manual_schedule(engines={mybir.EngineType.PE, mybir.EngineType.DVE}):
             for c in range(len(S_CHUNKS)):
+                if c == 2:
+                    quantise_u0_half(u0_grouped, first_half)
                 if c < SCALAR_CHUNKS:
                     regroup_s(c, "vector", 0, R_HALF)
                     regroup_s(c, "scalar", R_HALF, R_HALF)
                 else:
                     regroup_s(c, "vector", 0, R_HALF // 2)
                     regroup_s(c, "scalar", R_HALF // 2, R_HALF // 2)
+                if c == 2:
+                    for r in range(EARLY_R):
+                        quantise_s_part(r, 0)
                 if c in WARM_UP:
                     warm_up(c, WARM_UP[c])
                 if c == 0:
-                    quantise_u0_half(first_half)
-            quantise_s(0)
+                    u0_grouped = turn_factor(
+                        nc,
+                        psum,
+                        "one",
+                        stage,
+                        identity[:],
+                        u0_rows[:, first_half, :],
+                        (nc.vector.tensor_copy, nc.vector.tensor_copy),
+                    )
+            for r in range(EARLY_R):
+                quantise_s_part(r, Y_PART)
             for n in range(UNIT):
                 contraction_step(n)
-            quantise_factor(
-                nc, psum, "two", stage, identity[:], u1_rows[:], u1_codes[:], u1_scales[:]
+            u1_grouped = turn_factor(nc, psum, "two", stage, identity[:], u1_rows[:], both)
+            quantise_w1(0)
+            nc.vector.quantize_mx(
+                out=u1_codes[:].bitcast(FP8X4), scales=u1_scales[:], in_=u1_grouped[:]
             )
 
-        for n in range(UNIT, BANKS + LAG):
+        with tc.manual_schedule(engines={mybir.EngineType.PE}):
+            for n in range(UNIT, U0_SECOND + 1):
+                contraction_step(n)
+        for n in range(U0_SECOND + 1, BANKS + LAG):
             contraction_step(n)

from contextlib import ExitStack

import concourse.mybir as mybir
from concourse.masks import make_identity

BF16 = mybir.dt.bfloat16
F32 = mybir.dt.float32
U32 = mybir.dt.uint32
U8 = mybir.dt.uint8
FP8X4 = mybir.dt.float8_e4m3fn_x4

P = 128
PACK = 4
K = P * PACK
R = 8
J = 1024
I = 512
J_BLOCKS = J // P
FACTOR_BLOCKS = 4
R_HALF = R // 2
S_CHUNKS = (128, 128, 128, 128)
UNIT = 4
SCALAR_CHUNKS = 3
Y_PART = P // 2
EARLY_R = 2
U0_SECOND = 11
WARM_UP_COLUMNS = 512
WARM_UP = {2: 5, 3: 3}
STORE_BANKS = 2
STORES_IN_FLIGHT = 8
BANKS = R * J_BLOCKS
UNIT_LAST = list(range(UNIT - 1, BANKS, UNIT))
PSUM_BANKS = 8
LAG = 8
SCALAR_SHARE = 4
SCALAR_EARLY = (1, 3, 4, 5)

FLOPS = 2 * K * (K * R) * J + 2 * K * (R * J) * I


def unit_indices(n):
    unit = sum(1 for last in UNIT_LAST if last < n)
    first = UNIT_LAST[unit - 1] + 1 if unit > 0 else 0
    return unit, n - first, UNIT_LAST[unit] + 1 - first


def bank_indices(n):
    r_half, rest = divmod(n, BANKS // 2)
    j_half, rest = divmod(rest, BANKS // 4)
    r_low, place = divmod(rest, FACTOR_BLOCKS)
    return r_half * R_HALF + r_low, j_half * FACTOR_BLOCKS + place


def turn_factor(nc, psum, tag, stage, identity, rows, copies):
    grouped = stage.tile([P, FACTOR_BLOCKS * P * PACK], BF16, align_bytes=64, name="factor_grouped")
    grouped_words = grouped[:].bitcast(F32).rearrange("x (b a u) -> x b a u", b=FACTOR_BLOCKS, u=2)
    for first in range(0, FACTOR_BLOCKS, 2):
        flipped = psum.tile([P, 2, 2, P], F32, name="factor_flipped", tag=tag)
        for b in range(2):
            words = rows[:, first + b, :].bitcast(F32)
            for u in range(2):
                nc.tensor.transpose(flipped[:, b, u, :], words[:, u::2], identity)
        copy = copies[first // 2]
        copy(out=grouped_words[:, first : first + 2], in_=flipped[:].rearrange("x b u a -> x b a u"))
    return grouped


def tile_mtl_net_tf_pa_kernel(tc, S, U0, U1, out):
    nc = tc.nc
    with ExitStack() as ctx:
        keep = ctx.enter_context(tc.tile_pool(name="keep", bufs=1))
        stage = ctx.enter_context(tc.tile_pool(name="stage", bufs=3))
        psum = ctx.enter_context(tc.psum_pool(name="psum", bufs=PSUM_BANKS // 2))

        u0_view = U0.rearrange("(a b) q -> a b q", b=J_BLOCKS)
        u0_rows = keep.tile([P, J_BLOCKS, K], BF16)
        first_half = slice(0, FACTOR_BLOCKS)
        second_half = slice(FACTOR_BLOCKS, J_BLOCKS)
        u1_rows = keep.tile([P, FACTOR_BLOCKS, K], BF16)
        s_view = S.rearrange("(x t) p r -> x t p r", t=PACK)
        s_raw = []
        s_first = []
        for c, width in enumerate(S_CHUNKS):
            p0 = sum(S_CHUNKS[:c])
            raw = keep.tile([P, PACK, width, R], BF16, name="s_raw%d" % c)
            nc.sync.dma_start(out=raw[:], in_=s_view[:, :, p0 : p0 + width, :])
            s_raw.append(raw)
            s_first.append(p0)
            if c == 0:
                nc.sync.dma_start(out=u0_rows[:, first_half, :], in_=u0_view[:, first_half, :])
        nc.sync.dma_start(out=u1_rows[:], in_=U1.rearrange("(b a) p -> a b p", a=P))
        nc.sync.dma_start(out=u0_rows[:, second_half, :], in_=u0_view[:, second_half, :])

        identity = keep.tile([P, P], F32)
        make_identity(nc, identity[:])

        u0_codes = keep.tile([P, J_BLOCKS, P], U32, align_bytes=64)
        u0_scales = keep.tile([P, J_BLOCKS, P], U8, align_bytes=64)
        u1_codes = keep.tile([P, I], U32, align_bytes=64)
        u1_scales = keep.tile([P, I], U8, align_bytes=64)
        s_codes = keep.tile([P, R, PACK * P], U32, align_bytes=64)
        s_scales = keep.tile([P, R, PACK * P], U8, align_bytes=64)
        s_grouped = [
            keep.tile([P, R_HALF, PACK, P, PACK], BF16, align_bytes=64, name="s_grouped%d" % half)
            for half in range(2)
        ]
        w1_bank = {}
        w1_grouped = {}
        w1_codes = {}
        w1_scales = {}
        result = {}
        out_view = out.rearrange("r (a b) i -> r a b i", b=J_BLOCKS)

        def quantise_u0_half(grouped, blocks):
            nc.vector.quantize_mx(
                out=u0_codes[:, blocks, :].rearrange("x b a -> x (b a)").bitcast(FP8X4),
                scales=u0_scales[:, blocks, :].rearrange("x b a -> x (b a)"),
                in_=grouped[:],
            )

        def regroup_s(c, engine, r_first, r_count, k_first=0, k_count=PACK):
            half, r_low = divmod(r_first, R_HALF)
            y_run = slice(s_first[c] // PACK, (s_first[c] + S_CHUNKS[c]) // PACK)
            k_run = slice(k_first, k_first + k_count)
            target = s_grouped[half][:, r_low : r_low + r_count, k_run, y_run, :].rearrange(
                "x r k y t -> x k y t r"
            )
            source = s_raw[c][:, :, :, r_first : r_first + r_count].rearrange(
                "x t (y k) r -> x k y t r", k=PACK
            )[:, k_run]
            if engine == "vector":
                nc.vector.tensor_copy(out=target, in_=source)
            else:
                nc.scalar.copy(out=target, in_=source)

        def warm_up(c, count):
            idle_bank = psum.tile([P, WARM_UP_COLUMNS], F32, name="idle_bank", tag="two")
            for t in range(count):
                flat = s_raw[c][:, t % PACK].rearrange("x p r -> x (p r)")
                nc.tensor.matmul(
                    idle_bank[:],
                    lhsT=flat[:, :P],
                    rhs=flat[:, :WARM_UP_COLUMNS],
                    start=True,
                    stop=True,
                )

        def quantise_s(r):
            half, r_low = divmod(r, R_HALF)
            nc.vector.quantize_mx(
                out=s_codes[:, r, :].bitcast(FP8X4),
                scales=s_scales[:, r, :],
                in_=s_grouped[half][:, r_low].rearrange("x k y t -> x (k y t)"),
            )

        def quantise_s_part(r, y_first):
            half, r_low = divmod(r, R_HALF)
            for k in range(PACK):
                columns = slice(k * P + y_first, k * P + y_first + Y_PART)
                nc.vector.quantize_mx(
                    out=s_codes[:, r, columns].bitcast(FP8X4),
                    scales=s_scales[:, r, columns],
                    in_=s_grouped[half][:, r_low, k, y_first : y_first + Y_PART, :].rearrange(
                        "x y t -> x (y t)"
                    ),
                )

        def first_contraction(n):
            r, b = bank_indices(n)
            w1_bank[n] = psum.tile([P, PACK, P], F32, name="w1_bank", tag="one")
            for k in range(PACK):
                nc.tensor.matmul_mx(
                    out=w1_bank[n][:, k, :],
                    lhsT=s_codes[:, r, k * P : (k + 1) * P].bitcast(FP8X4),
                    lhsT_scale=s_scales[:, r, k * P : (k + 1) * P],
                    rhs=u0_codes[:, b, :].bitcast(FP8X4),
                    rhs_scale=u0_scales[:, b, :],
                    start=True,
                    stop=True,
                )

        def round_w1(n):
            unit, place, count = unit_indices(n)
            if place == 0:
                w1_grouped[unit] = stage.tile(
                    [P, count, P, PACK], BF16, align_bytes=64, name="w1_grouped"
                )
            source = w1_bank[n][:].rearrange("y k a -> y a k")
            if n >= UNIT:
                nc.any.tensor_copy(out=w1_grouped[unit][:, place], in_=source)
            elif n % 2 == 1:
                nc.scalar.copy(out=w1_grouped[unit][:, place], in_=source)
            else:
                nc.vector.tensor_copy(out=w1_grouped[unit][:, place], in_=source)

        def quantise_w1(unit):
            count = unit_indices(UNIT_LAST[unit])[2]
            w1_codes[unit] = stage.tile([P, count * P], U32, align_bytes=64, name="w1_codes")
            w1_scales[unit] = stage.tile([P, count * P], U8, align_bytes=64, name="w1_scales")
            nc.vector.quantize_mx(
                out=w1_codes[unit][:].bitcast(FP8X4),
                scales=w1_scales[unit][:],
                in_=w1_grouped[unit][:].rearrange("y u a k -> y (u a k)"),
            )

        def second_contraction(n):
            r, b = bank_indices(n)
            unit, place = unit_indices(n)[:2]
            batch, slot = divmod(n, STORE_BANKS)
            if slot == 0:
                result[batch] = stage.tile(
                    [P, STORE_BANKS, I], F32, name="result", bufs=STORES_IN_FLIGHT
                )
            out_bank = psum.tile([P, I], F32, name="out_bank", tag="two")
            nc.tensor.matmul_mx(
                out=out_bank[:],
                lhsT=w1_codes[unit][:, place * P : (place + 1) * P].bitcast(FP8X4),
                lhsT_scale=w1_scales[unit][:, place * P : (place + 1) * P],
                rhs=u1_codes[:].bitcast(FP8X4),
                rhs_scale=u1_scales[:],
                start=True,
                stop=True,
            )
            nc.any.tensor_copy(out=result[batch][:, slot, :], in_=out_bank[:])
            if slot == STORE_BANKS - 1:
                nc.sync.dma_start(out=out_view[r, :, b - slot : b + 1, :], in_=result[batch][:])

        both = (nc.vector.tensor_copy, nc.scalar.copy)

        def contraction_step(n):
            if n >= LAG:
                second_contraction(n - LAG)
            if n < BANKS:
                first_contraction(n)
                round_w1(n)
            if n - 1 in UNIT_LAST and n > UNIT:
                quantise_w1(UNIT_LAST.index(n - 1))
            if n % UNIT == 1 and UNIT < n < BANKS and bank_indices(n)[1] < FACTOR_BLOCKS:
                r_next = bank_indices(n)[0] + 1
                if r_next % R_HALF != 0:
                    quantise_s(r_next)
            if n == BANKS // 2 - 2 * UNIT:
                quantise_s(R_HALF)
            if 2 * UNIT <= n < 3 * UNIT:
                regroup_s(SCALAR_CHUNKS, "vector", R_HALF, R_HALF, n - 2 * UNIT, 1)
            if n == U0_SECOND:
                quantise_u0_half(
                    turn_factor(
                        nc, psum, "one", stage, identity[:], u0_rows[:, second_half, :], both
                    ),
                    second_half,
                )

        with tc.manual_schedule(engines={mybir.EngineType.PE, mybir.EngineType.DVE}):
            for c in range(len(S_CHUNKS)):
                if c == 2:
                    quantise_u0_half(u0_grouped, first_half)
                if c < SCALAR_CHUNKS:
                    regroup_s(c, "vector", 0, R_HALF)
                    regroup_s(c, "scalar", R_HALF, R_HALF)
                else:
                    regroup_s(c, "vector", 0, R_HALF // 2)
                    regroup_s(c, "scalar", R_HALF // 2, R_HALF // 2)
                if c == 2:
                    for r in range(EARLY_R):
                        quantise_s_part(r, 0)
                if c in WARM_UP:
                    warm_up(c, WARM_UP[c])
                if c == 0:
                    u0_grouped = turn_factor(
                        nc,
                        psum,
                        "one",
                        stage,
                        identity[:],
                        u0_rows[:, first_half, :],
                        (nc.vector.tensor_copy, nc.vector.tensor_copy),
                    )
            for r in range(EARLY_R):
                quantise_s_part(r, Y_PART)
            for n in range(UNIT):
                contraction_step(n)
            u1_grouped = turn_factor(nc, psum, "two", stage, identity[:], u1_rows[:], both)
            quantise_w1(0)
            nc.vector.quantize_mx(
                out=u1_codes[:].bitcast(FP8X4), scales=u1_scales[:], in_=u1_grouped[:]
            )

        with tc.manual_schedule(engines={mybir.EngineType.PE}):
            for n in range(UNIT, U0_SECOND + 1):
                contraction_step(n)
        for n in range(U0_SECOND + 1, BANKS + LAG):
            contraction_step(n)
